import numpy as np
import ml_dtypes


def mxq(x, axis, fmt="e4m3"):
    dtype, down = {"e4m3": (ml_dtypes.float8_e4m3fn, 7), "e5m2": (ml_dtypes.float8_e5m2, 14)}[fmt]
    v = np.moveaxis(np.asarray(x, np.float32).astype(ml_dtypes.bfloat16).astype(np.float64), axis, -1)
    blocks = v.reshape(v.shape[:-1] + (-1, 32))
    amax = np.abs(blocks).max(-1, keepdims=True)
    byte = np.maximum(np.where(amax > 0, np.frexp(amax)[1] - 1 + 127, 0) - down, 1)
    scale = np.exp2(byte - 127.0)
    codes = (blocks / scale).astype(np.float32).astype(dtype).astype(np.float64)
    return np.moveaxis((codes * scale).reshape(v.shape), -1, axis)


WIDE = False


def mx_kscale(k):
    if not WIDE:
        return np.ones(k)
    levels = np.array([18, -18])
    if k % 512:
        return np.exp2(np.random.permutation(np.resize(levels, k // 32))).repeat(32)
    a = np.empty((k // 512, 16))
    for p in range(k // 512):
        a[p, :8] = np.random.permutation(np.resize(levels, 8))
        for g in range(8):
            far = levels[np.abs(levels - a[p, g]) >= 10]
            a[p, g + 8] = far[np.random.randint(len(far))]
    return np.exp2(a.ravel()).repeat(32)


BF16 = ml_dtypes.bfloat16


def bf(x):
    return np.asarray(x, np.float32).astype(BF16)


def f64(x):
    return np.asarray(x).astype(np.float64)


B, S, D = 1, 1024, 1024


def sigmoid(z):
    return 1.0 / (1.0 + np.exp(-z))


def setup_inputs():
    s = mx_kscale(B * S).reshape(B, S, 1)
    u = mx_kscale(D)
    v = mx_kscale(D)
    x0 = bf(np.random.standard_normal((B, S, D)))
    wq_0 = bf(np.random.standard_normal((D, D)) / np.sqrt(D))
    wq_b = bf(np.random.standard_normal(D) * 0.1)
    r_aft = bf(np.random.standard_normal((B, S, D)) * 6.0 / np.sqrt(S))
    ow_0 = bf(np.random.standard_normal((D, D)) * 6.0 / np.sqrt(D))
    out_b = bf(np.random.standard_normal(D) * 0.1)
    g = bf(np.random.standard_normal((B, S, D)) * np.exp2(np.random.randint(-6, 1, (B, S, 1))) * 16.0 / s * u)
    q = f64(x0) @ f64(wq_0).T + f64(wq_b)
    return {
        'x': bf(f64(x0) * s),
        'wq_w': bf(f64(wq_0) / v[:, None]),
        'wq_b': wq_b,
        'r_aft': r_aft,
        'out_w': bf(f64(ow_0) * v[None, :] / u[:, None]),
        'out_b': out_b,
        'q': np.asarray(q, np.float32),
        'grad_out': g,
    }


def reference(x, wq_w, wq_b, r_aft, out_w, out_b, q, grad_out):
    g = f64(grad_out).reshape(B * S, D)
    xf = f64(x).reshape(B * S, D)
    rf = f64(r_aft).reshape(B * S, D)
    sg = sigmoid(f64(q).reshape(B * S, D))
    dy = mxq(g, 1, 'e5m2') @ mxq(f64(out_w), 0, 'e4m3')
    dq = dy * rf * sg * (1.0 - sg)
    dx = mxq(dq, 1, 'e5m2') @ mxq(f64(wq_w), 0, 'e4m3')
    dwq = mxq(dq, 0, 'e5m2').T @ mxq(xf, 0, 'e4m3')
    return dx.reshape(B, S, D), dwq

from contextlib import ExitStack

import concourse.mybir as mybir
from concourse.masks import make_identity

F32 = mybir.dt.float32
BF16 = mybir.dt.bfloat16
U32 = mybir.dt.uint32
U8 = mybir.dt.uint8
E4M3 = mybir.dt.float8_e4m3fn_x4
E5M2 = mybir.dt.float8_e5m2_x4
ALU = mybir.AluOpType
ACT = mybir.ActivationFunctionType

P = 128
D = 1024
PACK = 4
PASS = 512
N_PASS = D // PASS
N_HALF = D // 512
TILES = D // P
FLOPS = 3 * 2 * D * D * D
BYTES = 5 * 2 * D * D + 4 * D * D + 2 * 4 * D * D


CFG = {
    "FB": 2,
    "BB": 6,
    "PLAN": [
        ("Lg", 0, 0),
        ("fp", "g", 0),
        ("fp", "g", 1),
        ("Lw", "ow", 1, 1),
        ("Lw", "ow", 1, 0),
        ("fc", "g", 0, "v"),
        ("fc", "g", 1, "v"),
        ("fq", "g", 0),
        ("Lg", 0, 1),
        ("Lw", "ow", 0, 0),
        ("Lq", 1),
        ("Lw", "ow", 0, 1),
        ("fp", "g", 2),
        ("fq", "g", 1),
        ("Lq", 0),
        ("il", "ow", 1, 1, "s"),
        ("Lg", 1, 0),
        ("fp", "g", 3),
        ("Lr", 0, 0),
        ("il", "ow", 1, 0, "v"),
        ("Lq", 2),
        ("wq", "ow", 1, 1),
        ("wq", "ow", 1, 0),
        ("fc", "g", 2, "s"),
        ("fc", "g", 3, "s"),
        ("fp", "g", 4),
        ("fq", "g", 2),
        ("Lg", 1, 1),
        ("th", 1, 0),
        ("Lq", 3),
        ("th", 1, 1),
        ("sq", 1, 0),
        ("il", "ow", 0, 0, "v"),
        ("fp", "g", 5),
        ("sq", 1, 1),
        ("th", 0, 1),
        ("fq", "g", 3),
        ("il", "ow", 0, 1, "v"),
        ("wq", "ow", 0, 0),
        ("wq", "ow", 0, 1),
        ("th", 0, 0),
        ("sq", 0, 1),
        ("sq", 0, 0),
        ("fc", "g", 5, "s"),
        ("fc", "g", 4, "v"),
        ("w", 1, 1),
        ("dy", 0, 1),
        ("th", 2, 1),
        ("w", 0, 1),
        ("fq", "g", 4),
        ("th", 2, 0),
        ("sq", 2, 1),
        ("Lw", "wq", 0, 0),
        ("sq", 2, 0),
        ("dy", 1, 0),
        ("Lr", 0, 1),
        ("th", 3, 0),
        ("Lq", 4),
        ("dy", 0, 0),
        ("fq", "g", 5),
        ("w", 1, 0),
        ("fp", "g", 6),
        ("w", 0, 0),
        ("mul", 1, 0),
        ("fc", "g", 6, "v"),
        ("fp", "g", 7),
        ("mul", 0, 0),
        ("dy", 3, 0),
        ("th", 3, 1),
        ("dy", 2, 0),
        ("mul", 0, 1),
        ("fc", "g", 7, "s"),
        ("sq", 3, 0),
        ("wm", "wq", 0, 0, 1),
        ("sq", 3, 1),
        ("fq", "g", 6),
        ("dy", 2, 1),
        ("fq", "g", 7),
        ("Lw", "wq", 0, 1),
        ("w", 2, 0),
        ("wc", "wq", 0, 0, 1, "s"),
        ("w", 3, 0),
        ("Lw", "wq", 1, 0),
        ("mul", 2, 0),
        ("mul", 3, 0),
        ("wm", "wq", 0, 0, 0),
        ("w", 3, 1),
        ("Lr", 1, 0),
        ("th", 4, 0),
        ("dy", 3, 1),
        ("dy", 4, 0),
        ("wm", "wq", 0, 1, 1),
        ("dy", 4, 1),
        ("wc", "wq", 0, 0, 0, "s"),
        ("th", 4, 1),
        ("wq", "wq", 0, 0),
        ("sq", 4, 0),
        ("wm", "wq", 1, 0, 0),
        ("w", 2, 1),
        ("Lq", 7),
        ("wc", "wq", 0, 1, 1, "s"),
        ("sq", 4, 1),
        ("wc", "wq", 1, 0, 0, "s"),
        ("mul", 3, 1),
        ("mv", 0, 0),
        ("mc", 0, 0, "s"),
        ("th", 7, 0),
        ("w", 4, 1),
        ("Lq", 5),
        ("w", 4, 0),
        ("dy", 1, 1),
        ("wm", "wq", 0, 1, 0),
        ("mv", 0, 1),
        ("wc", "wq", 0, 1, 0, "s"),
        ("mq", 0, 0),
        ("dy", 5, 0),
        ("Lw", "wq", 1, 1),
        ("mul", 2, 1),
        ("mc", 0, 1, "s"),
        ("mul", 4, 1),
        ("wm", "wq", 1, 0, 1),
        ("th", 7, 1),
        ("th", 5, 0),
        ("Lq", 6),
        ("fp", "dq", 0, 1, 1),
        ("mul", 1, 1),
        ("wc", "wq", 1, 0, 1, "v"),
        ("fc", "dq", 0, 1, 1, "s"),
        ("mq", 0, 1),
        ("dy", 7, 0),
        ("Lr", 1, 1),
        ("wm", "wq", 1, 1, 0),
        ("sq", 5, 0),
        ("wc", "wq", 1, 1, 0, "s"),
        ("Lw", "x", 0, 1),
        ("mul", 4, 0),
        ("wq", "wq", 1, 0),
        ("th", 5, 1),
        ("w", 5, 0),
        ("fp", "dq", 0, 0, 0),
        ("fc", "dq", 0, 0, 0, "s"),
        ("Lw", "x", 1, 1),
        ("dy", 6, 0),
        ("fp", "dq", 0, 1, 0),
        ("fq", "dq", 0, 1, 1),
        ("fp", "dq", 0, 0, 1),
        ("mul", 5, 0),
        ("Lw", "x", 0, 0),
        ("th", 6, 0),
        ("dy", 7, 1),
        ("fq", "dq", 0, 0, 0),
        ("wq", "wq", 0, 1),
        ("fc", "dq", 0, 1, 0, "s"),
        ("sq", 7, 0),
        ("fc", "dq", 0, 0, 1, "v"),
        ("fq", "dq", 0, 1, 0),
        ("sq", 6, 0),
        ("w", 7, 0),
        ("w", 6, 0),
        ("wm", "wq", 1, 1, 1),
        ("sq", 5, 1),
        ("fp", "dq", 1, 0, 0),
        ("mul", 7, 0),
        ("wc", "wq", 1, 1, 1, "s"),
        ("wq", "wq", 1, 1),
        ("dx", 0, 0),
        ("sq", 7, 1),
        ("mul", 6, 0),
        ("th", 6, 1),
        ("dx", 1, 0),
        ("fc", "dq", 1, 0, 0, "s"),
        ("em", "o0", 1, 0, "v"),
        ("dx", 1, 1),
        ("dx", 0, 1),
        ("Lw", "x", 1, 0),
        ("em", "o0", 1, 1, "s"),
        ("dy", 5, 1),
        ("em", "o0", 0, 0, "s"),
        ("w", 7, 1),
        ("fq", "dq", 0, 0, 1),
        ("mul", 7, 1),
        ("sq", 6, 1),
        ("mv", 1, 0),
        ("em", "o0", 0, 1, "v"),
        ("mc", 1, 0, "s"),
        ("mv", 1, 1),
        ("dx", 3, 1),
        ("dx", 2, 0),
        ("dx", 2, 1),
        ("il", "x", 0, 0, "s"),
        ("w", 5, 1),
        ("fq", "dq", 1, 0, 0),
        ("mul", 5, 1),
        ("fp", "dq", 1, 1, 0),
        ("mc", 1, 1, "v"),
        ("em", "o0", 2, 0, "v"),
        ("fc", "dq", 1, 1, 0, "v"),
        ("mv", 0, 3),
        ("w", 6, 1),
        ("em", "o0", 2, 1, "s"),
        ("fq", "dq", 1, 1, 0),
        ("em", "o0", 3, 1, "s"),
        ("dx", 3, 0),
        ("st", "o0", 1),
        ("dy", 6, 1),
        ("st", "o0", 0),
        ("em", "o0", 3, 0, "v"),
        ("mc", 0, 3, "s"),
        ("mul", 6, 1),
        ("il", "x", 1, 0, "s"),
        ("dx", 4, 1),
        ("mq", 1, 1),
        ("dx", 4, 0),
        ("dx", 5, 0),
        ("mv", 1, 3),
        ("wq", "x", 0, 0),
        ("mc", 1, 3, "s"),
        ("em", "o0", 4, 1, "v"),
        ("il", "x", 1, 1, "s"),
        ("mq", 1, 0),
        ("fp", "dq", 1, 0, 1),
        ("em", "o0", 5, 0, "s"),
        ("wq", "x", 1, 0),
        ("il", "x", 0, 1, "v"),
        ("dx", 5, 1),
        ("em", "o0", 4, 0, "v"),
        ("mv", 1, 2),
        ("wq", "x", 0, 1),
        ("wq", "x", 1, 1),
        ("dw", 1, 0),
        ("dw", 2, 0),
        ("em", "o1", 1, 0, "v"),
        ("dw", 3, 0),
        ("mq", 0, 3),
        ("dw", 0, 0),
        ("st", "o0", 2),
        ("fc", "dq", 1, 0, 1, "v"),
        ("em", "o0", 5, 1, "s"),
        ("dw", 1, 1),
        ("dw", 2, 1),
        ("em", "o1", 2, 1, "v"),
        ("st", "o0", 3),
        ("mq", 1, 3),
        ("mc", 1, 2, "s"),
        ("em", "o1", 1, 1, "s"),
        ("dw", 0, 1),
        ("em", "o1", 3, 0, "s"),
        ("em", "o1", 2, 0, "s"),
        ("st", "o0", 4),
        ("fp", "dq", 1, 1, 1),
        ("mv", 0, 2),
        ("em", "o1", 0, 0, "v"),
        ("fq", "dq", 1, 0, 1),
        ("dw", 3, 1),
        ("mq", 1, 2),
        ("st", "o0", 5),
        ("em", "o1", 0, 1, "s"),
        ("mc", 0, 2, "v"),
        ("st", "o1", 1),
        ("dw", 6, 0),
        ("dw", 6, 1),
        ("dw", 7, 1),
        ("fc", "dq", 1, 1, 1, "s"),
        ("em", "o1", 6, 0, "s"),
        ("em", "o1", 3, 1, "v"),
        ("dw", 7, 0),
        ("mq", 0, 2),
        ("st", "o1", 2),
        ("em", "o1", 6, 1, "s"),
        ("dw", 5, 1),
        ("em", "o1", 7, 0, "s"),
        ("st", "o1", 0),
        ("dw", 5, 0),
        ("st", "o1", 3),
        ("em", "o1", 5, 1, "s"),
        ("fq", "dq", 1, 1, 1),
        ("st", "o1", 6),
        ("em", "o1", 7, 1, "v"),
        ("st", "o1", 7),
        ("dw", 4, 1),
        ("dw", 4, 0),
        ("em", "o1", 5, 0, "s"),
        ("dx", 7, 0),
        ("dx", 7, 1),
        ("dx", 6, 0),
        ("em", "o1", 4, 0, "s"),
        ("st", "o1", 5),
        ("em", "o1", 4, 1, "v"),
        ("em", "o0", 7, 1, "s"),
        ("dx", 6, 1),
        ("em", "o0", 6, 0, "s"),
        ("em", "o0", 7, 0, "v"),
        ("st", "o1", 4),
        ("em", "o0", 6, 1, "s"),
        ("st", "o0", 7),
        ("st", "o0", 6),
    ],
}


def tile_aft_full_pb_v_kernel(
    tc, x, wq_w, wq_b, r_aft, out_w, out_b, q, grad_out, out_0, out_1
):
    nc = tc.nc
    with ExitStack() as ctx:
        keep = ctx.enter_context(tc.tile_pool(name="keep", bufs=1))
        work = ctx.enter_context(tc.tile_pool(name="work", bufs=2))
        psum = ctx.enter_context(tc.psum_pool(name="psum", bufs=2))

        ident = keep.tile([P, P], F32, name="ident")
        ident_bf = keep.tile([P, P], BF16, name="ident_bf")
        make_identity(nc, ident[:])
        make_identity(nc, ident_bf[:])

        def tokens(t):
            return t[0, :, :].rearrange("(g p j) w -> p g j w", p=P, j=PACK)

        def rows(t):
            return t.rearrange("(g p j) w -> p g j w", p=P, j=PACK)

        g_dram, q_dram, r_dram, x_dram = tokens(grad_out), tokens(q), tokens(r_aft), tokens(x)
        ow_dram, wq_dram = rows(out_w), rows(wq_w)
        out0_dram = tokens(out_0)

        g_raw, r_raw, q_sb, w_raw = {}, {}, {}, {}

        def load_pair(store, dram, g, pair, label):
            t = work.tile([P, 2, D], BF16, name="page", bufs=16)
            nc.sync.dma_start(out=t[:], in_=dram[:, g, 2 * pair : 2 * pair + 2, :])
            store[g, pair] = t

        def load_q(tt):
            t = work.tile([P, D], F32, name="page", bufs=16)
            nc.sync.dma_start(out=t[:], in_=q_dram[:, tt // 4, tt % 4, :])
            q_sb[tt] = t

        def load_w(label, dram, k, h):
            t = work.tile([P, PACK, 512], BF16, name="w_raw", bufs=12)
            nc.sync.dma_start(out=t[:], in_=dram[:, k, :, 512 * h : 512 * (h + 1)])
            w_raw[label, k, h] = t[:]

        def load_w2(label, dram, k):
            t = keep.tile([P, PACK, D], BF16, name="w_raw_%s%d" % (label, k))
            nc.sync.dma_start(out=t[:], in_=dram[:, k, :, :])
            for h in range(2):
                w_raw[label, k, h] = t[:, :, 512 * h : 512 * (h + 1)]

        codes, scales = {}, {}
        for label in ("ow", "wq", "x"):
            codes[label] = keep.tile([P, N_PASS, D], U32, name=label + "_codes", align_bytes=64)
            scales[label] = keep.tile([P, N_PASS, D], U8, name=label + "_scales", align_bytes=64)
        dq_codes = keep.tile([P, N_PASS, D], U32, name="dq_codes", align_bytes=64)
        dq_scales = keep.tile([P, N_PASS, D], U8, name="dq_scales", align_bytes=64)
        dq = [keep.tile([P, PACK, D], BF16, name="dq_%d" % g, align_bytes=64) for g in range(2)]

        grouped_w = {}

        def interleave(label, k, h, eng="v"):
            t = work.tile([P, 512, PACK], BF16, name="w_grouped", bufs=4, align_bytes=64)
            src = w_raw[label, k, h]
            copy = nc.scalar.copy if eng == "s" else nc.vector.tensor_copy
            copy(
                out=t[:].rearrange("p (c i) t -> p c t i", i=4),
                in_=src.rearrange("p t (c i) -> p c t i", i=4),
            )
            grouped_w[label, k, h] = t

        w_moved = {}

        def w_move(label, k, h, c):
            src = w_raw[label, k, h]
            ps = psum.tile([P, 256, PACK], BF16, name="flip_ps", bufs=FB)
            for b in range(2):
                f0 = 256 * c + 128 * b
                nc.tensor.matmul(
                    out=ps[:, 128 * b : 128 * (b + 1), :], lhsT=ident_bf[:],
                    rhs=src[:, :, f0 : f0 + 128].rearrange("p j w -> p w j"), start=True, stop=True,
                )
            w_moved[label, k, h, c] = ps

        def w_move_copy(label, k, h, c, eng="s"):
            if (label, k, h) not in grouped_w:
                t = work.tile([P, 512, PACK], BF16, name="w_grouped", bufs=4, align_bytes=64)
                grouped_w[label, k, h] = t
            t = grouped_w[label, k, h]
            copy = nc.scalar.copy if eng == "s" else nc.vector.tensor_copy
            copy(out=t[:, 256 * c : 256 * (c + 1), :].rearrange("p w t -> p (w t)"),
                 in_=w_moved[label, k, h, c][:].rearrange("p w t -> p (w t)"))

        def quant_w(label, k, h):
            cols = slice(512 * h, 512 * (h + 1))
            nc.vector.quantize_mx(
                out=codes[label][:, k, cols].bitcast(E4M3),
                scales=scales[label][:, k, cols],
                in_=grouped_w[label, k, h][:].rearrange("p w t -> p (w t)"),
            )

        FB, BB = CFG.get("FB", 2), CFG.get("BB", 6)
        flips = {}

        def flip_pe(key, blocks):
            ps = psum.tile([P, 2, 2, P], F32, name="flip_ps", bufs=FB)
            for a, words in enumerate(blocks):
                for u in range(2):
                    nc.tensor.transpose(ps[:, a, u, :], words[:, u : 256 : 2], ident[:])
            flips[key] = ps

        def flip_copy(key, eng="s"):
            t = work.tile([P, 2 * P * PACK], BF16, name=key[0] + "_flipped", bufs=3, align_bytes=64)
            copy = nc.scalar.copy if eng == "s" else nc.vector.tensor_copy
            copy(
                out=t[:].bitcast(F32).rearrange("p (a r u) -> p a r u", a=2, u=2),
                in_=flips[key][:].rearrange("p a u r -> p a r u"),
            )
            flips[key] = t

        def flip_quant(key):
            c = work.tile([P, 2 * P], U32, name=key[0] + "_fcodes", bufs=8, align_bytes=64)
            s = work.tile([P, 2 * P], U8, name=key[0] + "_fscales", bufs=8, align_bytes=64)
            nc.vector.quantize_mx(out=c[:].bitcast(E5M2), scales=s[:], in_=flips[key][:])
            flips[key] = (c, s)

        def g_blocks(tt):
            words = g_raw[tt // 4, (tt % 4) // 2][:, tt % 2, :].bitcast(F32)
            return [words[:, 256 * k : 256 * (k + 1)] for k in range(2)]

        def dq_blocks(g, h, pair):
            return [dq[g][:, 2 * pair + a, 512 * h : 512 * (h + 1)].bitcast(F32) for a in range(2)]

        def tanh(tt, h):
            cols = slice(512 * h, 512 * (h + 1))
            nc.scalar.activation(out=q_sb[tt][:, cols], in_=q_sb[tt][:, cols], func=ACT.Tanh, scale=0.5)

        def square(tt, h):
            cols = slice(512 * h, 512 * (h + 1))
            nc.scalar.activation(out=q_sb[tt][:, cols], in_=q_sb[tt][:, cols], func=ACT.Square, scale=0.5)

        def gate_w(tt, h):
            g, j = tt // 4, tt % 4
            cols = slice(512 * h, 512 * (h + 1))
            nc.vector.scalar_tensor_tensor(
                out=q_sb[tt][:, cols], in0=q_sb[tt][:, cols], scalar=0.25, in1=r_raw[g, j // 2][:, j % 2, cols],
                op0=ALU.subtract, op1=ALU.mult,
            )

        banks = {}

        def product(key, h, lhs, label):
            bank = psum.tile([P, 512], F32, name="bank", bufs=BB)
            cols = slice(512 * h, 512 * (h + 1))
            for k in range(N_PASS):
                c, s = lhs(k)
                nc.tensor.matmul_mx(
                    out=bank[:], lhsT=c.bitcast(E5M2), lhsT_scale=s,
                    rhs=codes[label][:, k, cols].bitcast(E4M3), rhs_scale=scales[label][:, k, cols],
                    start=(k == 0), stop=(k == N_PASS - 1),
                )
            banks[key, h] = bank

        def dy(tt, h):
            def lhs(k):
                c, s = flips["g", tt]
                return c[:, P * k : P * (k + 1)], s[:, P * k : P * (k + 1)]
            product(("dy", tt), h, lhs, "ow")

        def dx(tt, h):
            g, j = tt // 4, tt % 4
            def lhs(k):
                c, s = flips["dq", g, k, j // 2]
                a = j % 2
                return c[:, P * a : P * (a + 1)], s[:, P * a : P * (a + 1)]
            product(("o0", tt), h, lhs, "wq")

        def dw(m, h):
            cols = slice(P * m, P * (m + 1))
            product(("o1", m), h, lambda k: (dq_codes[:, k, cols], dq_scales[:, k, cols]), "x")

        def dq_mul(tt, h):
            g, j = tt // 4, tt % 4
            cols = slice(512 * h, 512 * (h + 1))
            nc.vector.scalar_tensor_tensor(
                out=dq[g][:, j, cols], in0=banks[("dy", tt), h][:], scalar=-1.0, in1=q_sb[tt][:, cols],
                op0=ALU.mult, op1=ALU.mult,
            )

        outs = {}

        def emit(kind, n, h, eng="s"):
            key = kind, n
            if key not in outs:
                t = work.tile([P, D], F32, name="page", bufs=16)
                outs[key] = t
            copy = nc.scalar.copy if eng == "s" else nc.vector.tensor_copy
            copy(out=outs[key][:, 512 * h : 512 * (h + 1)], in_=banks[key, h][:])

        def store(kind, n):
            dram = out0_dram[:, n // 4, n % 4, :] if kind == "o0" else out_1[P * n : P * (n + 1), :]
            nc.sync.dma_start(out=dram, in_=outs[kind, n][:])

        moved = {}

        def move(g, c):
            ps = psum.tile([P, 256, PACK], BF16, name="flip_ps", bufs=FB)
            for b in range(2):
                f0 = 256 * c + 128 * b
                nc.tensor.matmul(
                    out=ps[:, 128 * b : 128 * (b + 1), :], lhsT=ident_bf[:],
                    rhs=dq[g][:, :, f0 : f0 + 128].rearrange("p j w -> p w j"), start=True, stop=True,
                )
            moved[g, c] = ps

        def move_copy(g, c, eng="s"):
            t = work.tile([P, 256, PACK], BF16, name="dq_grouped", bufs=4, align_bytes=64)
            copy = nc.scalar.copy if eng == "s" else nc.vector.tensor_copy
            copy(out=t[:].rearrange("p w t -> p (w t)"), in_=moved[g, c][:].rearrange("p w t -> p (w t)"))
            moved[g, c] = t

        def move_v(g, c, eng="v"):
            t = work.tile([P, 256, PACK], BF16, name="dq_grouped", bufs=4, align_bytes=64)
            copy = nc.scalar.copy if eng == "s" else nc.vector.tensor_copy
            copy(
                out=t[:].rearrange("p (c i) t -> p c t i", i=4),
                in_=dq[g][:, :, 256 * c : 256 * (c + 1)].rearrange("p t (c i) -> p c t i", i=4),
            )
            moved[g, c] = t

        def move_quant(g, c):
            cols = slice(256 * c, 256 * (c + 1))
            nc.vector.quantize_mx(out=dq_codes[:, g, cols].bitcast(E5M2), scales=dq_scales[:, g, cols],
                in_=moved[g, c][:].rearrange("p w t -> p (w t)"))


        def f_pe(*key):
            flip_pe(key, g_blocks(key[1]) if key[0] == "g" else dq_blocks(*key[1:]))

        def f_copy(*a):
            flip_copy(a[:-1], a[-1])

        def f_quant(*key):
            flip_quant(key)

        DR = {"ow": ow_dram, "wq": wq_dram, "x": x_dram}
        FUNCS = {
            "Lg": lambda g, p: load_pair(g_raw, g_dram, g, p, "g"), "Lr": lambda g, p: load_pair(r_raw, r_dram, g, p, "r"),
            "Lq": load_q, "Lw": lambda l, k, h: load_w(l, DR[l], k, h),
            "fp": f_pe, "fc": f_copy, "fq": f_quant, "dy": dy, "mul": dq_mul, "th": tanh, "sq": square, "w": gate_w,
            "il": interleave, "wm": w_move, "wc": w_move_copy, "wq": quant_w, "mv": move, "mc": move_copy, "mV": move_v, "mq": move_quant,
            "dx": dx, "dw": dw, "em": emit, "st": store,
        }
        with tc.manual_schedule():
            for tok in CFG["PLAN"]:
                FUNCS[tok[0]](*tok[1:])
